import numpy as np
import ml_dtypes


def mxq(x, axis, fmt="e4m3"):
    dtype, down = {"e4m3": (ml_dtypes.float8_e4m3fn, 7), "e5m2": (ml_dtypes.float8_e5m2, 14)}[fmt]
    v = np.moveaxis(np.asarray(x, np.float32).astype(ml_dtypes.bfloat16).astype(np.float64), axis, -1)
    blocks = v.reshape(v.shape[:-1] + (-1, 32))
    amax = np.abs(blocks).max(-1, keepdims=True)
    byte = np.maximum(np.where(amax > 0, np.frexp(amax)[1] - 1 + 127, 0) - down, 1)
    scale = np.exp2(byte - 127.0)
    codes = (blocks / scale).astype(np.float32).astype(dtype).astype(np.float64)
    return np.moveaxis((codes * scale).reshape(v.shape), -1, axis)


WIDE = False


def mx_kscale(k):
    if not WIDE:
        return np.ones(k)
    levels = np.array([10, -10, 5, -5, 0])
    if k % 512:
        return np.exp2(np.random.permutation(np.resize(levels, k // 32))).repeat(32)
    a = np.empty((k // 512, 16))
    for p in range(k // 512):
        a[p, :8] = np.random.permutation(np.resize(levels, 8))
        for g in range(8):
            far = levels[np.abs(levels - a[p, g]) >= 10]
            a[p, g + 8] = far[np.random.randint(len(far))]
    return np.exp2(a.ravel()).repeat(32)


BF16 = ml_dtypes.bfloat16


def bf(x):
    return np.asarray(x, np.float32).astype(BF16)


def f64(x):
    return np.asarray(x).astype(np.float64)


B, S, D, DFF, R = 4, 2048, 512, 1024, 512


def setup_inputs():
    t, r = mx_kscale(DFF), mx_kscale(R)
    v = np.random.standard_normal((B, S, DFF)) * 1.2
    return {"h_gelu": bf(v / (1.0 + np.exp(-1.702 * v)) * t),
            "c_proj_U": bf(np.random.standard_normal((DFF, R)) * 2.0 / np.sqrt(DFF) / t[:, None]),
            "c_proj_S": bf(np.random.uniform(size=R) * r),
            "c_proj_V": bf(np.random.standard_normal((D, R)) / np.sqrt(R) / r[None, :]),
            "c_proj_bias": bf(np.random.standard_normal(D) * 0.3)}


def reference(h_gelu, c_proj_U, c_proj_S, c_proj_V, c_proj_bias):
    us = f64(c_proj_U) * f64(c_proj_S)[None, :]
    w = mxq(us, 1, "e4m3") @ mxq(f64(c_proj_V), 1, "e4m3").T
    return (mxq(f64(h_gelu), 2, "e4m3") @ mxq(w, 0, "e4m3")) + f64(c_proj_bias)

@@ -1,0 +1,243 @@
+from contextlib import ExitStack
+
+import concourse.mybir as mybir
+from concourse.masks import make_identity
+
+F32 = mybir.dt.float32
+BF16 = mybir.dt.bfloat16
+U32 = mybir.dt.uint32
+U8 = mybir.dt.uint8
+FP8X4 = mybir.dt.float8_e4m3fn_x4
+MULT = mybir.AluOpType.mult
+ADD = mybir.AluOpType.add
+
+P = 128
+PACK = 4
+TOKENS = 4 * 2048
+DFF = 1024
+R = 512
+D = 512
+
+BANK = 512
+PLANES = DFF // P
+PASSES = DFF // (P * PACK)
+TILES = 4
+CHUNK = TILES * P
+N_CHUNKS = TOKENS // CHUNK
+
+LOOKAHEAD = 2
+H_BUFS = 8
+
+FLOPS = 2 * DFF * R * D + 2 * TOKENS * DFF * D
+
+
+def tile_hybridsuperlayer_pb_t_kernel(
+    tc, h_gelu, c_proj_U, c_proj_S, c_proj_V, c_proj_bias, out
+):
+    nc = tc.nc
+    h_chunks = h_gelu.flatten_outer_dims().rearrange("(c p i) k -> c p (i k)", p=P, i=TILES)
+    out_chunks = out.flatten_outer_dims().rearrange("(c p i) d -> c p (i d)", p=P, i=TILES)
+
+    with ExitStack() as ctx:
+        ctx.enter_context(tc.manual_schedule())
+        const = ctx.enter_context(tc.tile_pool(name="const", bufs=1))
+        weights = ctx.enter_context(tc.tile_pool(name="weights", bufs=1))
+        h_pool = ctx.enter_context(tc.tile_pool(name="h", bufs=H_BUFS))
+        grouped_pool = ctx.enter_context(tc.tile_pool(name="grouped", bufs=3))
+        codes_pool = ctx.enter_context(tc.tile_pool(name="codes", bufs=LOOKAHEAD + 2))
+        out_pool = ctx.enter_context(tc.tile_pool(name="outs", bufs=4))
+        xt_pool = ctx.enter_context(tc.psum_pool(name="xt", bufs=4))
+        acc_pool = ctx.enter_context(tc.psum_pool(name="acc", bufs=4))
+
+        ident = const.tile([P, P], F32)
+        make_identity(nc, ident[:])
+        ones = const.tile([P, P], BF16)
+        nc.vector.memset(ones[:], 1.0)
+        bias_rows = const.tile([P, D], BF16)
+        nc.vector.memset(bias_rows[:], 0.0)
+
+        s_quad = const.tile([P, PACK], BF16)
+        nc.sync.dma_start(out=s_quad[:], in_=c_proj_S.rearrange("(q t) -> q t", t=PACK))
+
+        u_sb = weights.tile([P, PLANES * R], BF16)
+        u_view = u_sb[:].rearrange("p (c x) -> p c x", c=4)
+        u_dram = c_proj_U.rearrange("(g p h e) r -> g h p (e r)", g=PASSES, h=2, e=2)
+        for c in range(4):
+            nc.sync.dma_start(out=u_view[:, c, :], in_=u_dram[c // 2, c % 2])
+        v_sb = weights.tile([P, (D // P) * R], BF16)
+        nc.sync.dma_start(
+            out=v_sb[:].rearrange("p (t r) -> p t r", r=R),
+            in_=c_proj_V.rearrange("(t p) r -> p t r", p=P),
+        )
+        nc.sync.dma_start(out=bias_rows[0:1, :], in_=c_proj_bias.rearrange("(o d) -> o d", o=1))
+
+        h_tiles = {}
+
+        def load_chunk(c):
+            h_sb = h_pool.tile([P, TILES * DFF], BF16)
+            nc.sync.dma_start(out=h_sb[:], in_=h_chunks[c])
+            h_tiles[c] = h_sb
+
+        for c in range(H_BUFS):
+            load_chunk(c)
+
+        u_words = u_sb[:].bitcast(F32)
+        us_grouped = weights.tile([P, PLANES * P * PACK], BF16, align_bytes=64)
+        s_repeated = (
+            s_quad[:].rearrange("q (a b) -> q a b", b=2).unsqueeze(1).to_broadcast([P, P, 2, 2])
+        )
+        for c in range(PLANES // 2):
+            ut = xt_pool.tile([P, BANK], F32, tag="xt")
+            for e in range(2):
+                for a in range(2):
+                    nc.tensor.transpose(
+                        ut[:, (2 * e + a) * P : (2 * e + a + 1) * P],
+                        u_words[:, 256 * (2 * c + e) + a : 256 * (2 * c + e + 1) : 2],
+                        ident[:],
+                    )
+            ut_pairs = ut[:].bitcast(BF16).rearrange("q (e a m b) -> q e m a b", e=2, a=2, b=2)
+            for e in range(2):
+                j = 2 * c + e
+                nc.vector.tensor_tensor(
+                    out=us_grouped[:, j * P * PACK : (j + 1) * P * PACK].rearrange(
+                        "q (m a b) -> q m a b", a=2, b=2
+                    ),
+                    in0=ut_pairs[:, e],
+                    in1=s_repeated,
+                    op=MULT,
+                )
+
+        v_words = v_sb[:].bitcast(F32)
+        v_grouped = weights.tile([P, D * PACK], BF16, align_bytes=64)
+        v_grouped_words = v_grouped[:].bitcast(F32).rearrange("q (d a) -> q d a", a=2)
+        for half in range(2):
+            vt = xt_pool.tile([P, BANK], F32, tag="xt")
+            for a in range(2):
+                for s in range(2):
+                    t = 2 * half + s
+                    nc.tensor.transpose(
+                        vt[:, (2 * a + s) * P : (2 * a + s + 1) * P],
+                        v_words[:, 256 * t + a : 256 * (t + 1) : 2],
+                        ident[:],
+                    )
+            nc.scalar.copy(
+                out=v_grouped_words[:, half * 256 : (half + 1) * 256, :],
+                in_=vt[:].rearrange("q (a d) -> q d a", a=2),
+            )
+
+        v_codes = weights.tile([P, D], U32, align_bytes=64)
+        v_scales = weights.tile([P, D], U8, align_bytes=64)
+        nc.vector.quantize_mx(out=v_codes[:].bitcast(FP8X4), scales=v_scales[:], in_=v_grouped[:])
+        us_codes = weights.tile([P, PLANES * P], U32, align_bytes=64)
+        us_scales = weights.tile([P, PLANES * P], U8, align_bytes=64)
+        for g in range(PASSES):
+            nc.vector.quantize_mx(
+                out=us_codes[:, g * PACK * P : (g + 1) * PACK * P].bitcast(FP8X4),
+                scales=us_scales[:, g * PACK * P : (g + 1) * PACK * P],
+                in_=us_grouped[:, g * PACK * P * PACK : (g + 1) * PACK * P * PACK],
+            )
+
+        grouped_tiles = {}
+        code_tiles = {}
+
+        def transpose_chunk(c):
+            h_words = h_tiles[c][:].bitcast(F32)
+            grouped = grouped_pool.tile([P, CHUNK * PASSES * PACK], BF16, align_bytes=64)
+            grouped_words = grouped[:].bitcast(F32).rearrange(
+                "q (i g m u) -> q i g m u", i=TILES, g=PASSES, u=2
+            )
+            for i in range(TILES):
+                xt = xt_pool.tile([P, BANK], F32, tag="xt")
+                for w in range(BANK // P):
+                    first = 512 * i + 256 * (w // 2)
+                    nc.tensor.transpose(
+                        xt[:, w * P : (w + 1) * P],
+                        h_words[:, first + w % 2 : first + 256 : 2],
+                        ident[:],
+                    )
+                nc.scalar.copy(
+                    out=grouped_words[:, i],
+                    in_=xt[:].rearrange("q (g u m) -> q g m u", g=PASSES, u=2),
+                )
+            grouped_tiles[c] = grouped
+            if c + H_BUFS < N_CHUNKS:
+                load_chunk(c + H_BUFS)
+
+        def quantise_chunk(c):
+            h_codes = codes_pool.tile([P, CHUNK * PASSES], U32, align_bytes=64)
+            h_scales = codes_pool.tile([P, CHUNK * PASSES], U8, align_bytes=64)
+            nc.vector.quantize_mx(
+                out=h_codes[:].bitcast(FP8X4), scales=h_scales[:], in_=grouped_tiles[c][:]
+            )
+            code_tiles[c] = (h_codes, h_scales)
+
+        def multiply_chunk(c):
+            h_codes, h_scales = code_tiles[c]
+            out_sb = out_pool.tile([P, TILES * D], F32)
+            for i in range(TILES):
+                acc = acc_pool.tile([P, D], F32, tag="acc")
+                for g in range(PASSES):
+                    tokens = slice((PASSES * i + g) * P, (PASSES * i + g + 1) * P)
+                    features = slice(g * D, (g + 1) * D)
+                    nc.tensor.matmul_mx(
+                        out=acc[:],
+                        lhsT=h_codes[:, tokens].bitcast(FP8X4),
+                        lhsT_scale=h_scales[:, tokens],
+                        rhs=w_codes[:, features].bitcast(FP8X4),
+                        rhs_scale=w_scales[:, features],
+                        start=(g == 0),
+                        stop=(g == PASSES - 1),
+                    )
+                nc.vector.tensor_tensor(
+                    out=out_sb[:, i * D : (i + 1) * D], in0=acc[:], in1=bias_bc[:], op=ADD
+                )
+            nc.sync.dma_start(out=out_chunks[c], in_=out_sb[:])
+
+        transpose_chunk(0)
+
+        bias_ps = acc_pool.tile([P, D], F32, tag="acc")
+        nc.tensor.matmul(out=bias_ps[:], lhsT=ones[:], rhs=bias_rows[:], start=True, stop=True)
+        bias_bc = const.tile([P, D], F32)
+        nc.scalar.copy(out=bias_bc[:], in_=bias_ps[:])
+
+        w_grouped = weights.tile([P, PASSES * D * PACK], BF16, align_bytes=64)
+        for g in range(PASSES):
+            for block in range(D // P):
+                w_ps = acc_pool.tile([P, BANK], F32, tag="acc")
+                for t in range(PACK):
+                    j = PACK * g + t
+                    nc.tensor.matmul_mx(
+                        out=w_ps[:, t * P : (t + 1) * P],
+                        lhsT=us_codes[:, j * P : (j + 1) * P].bitcast(FP8X4),
+                        lhsT_scale=us_scales[:, j * P : (j + 1) * P],
+                        rhs=v_codes[:, block * P : (block + 1) * P].bitcast(FP8X4),
+                        rhs_scale=v_scales[:, block * P : (block + 1) * P],
+                        start=True,
+                        stop=True,
+                    )
+                first = (g * (D // P) + block) * BANK
+                words_out = w_grouped[:, first : first + BANK].rearrange("p (d t) -> p d t", t=PACK)
+                planes_in = w_ps[:].rearrange("p (t d) -> p d t", t=PACK)
+                if block % 2 == 0:
+                    nc.scalar.copy(out=words_out, in_=planes_in)
+                else:
+                    nc.vector.tensor_copy(out=words_out, in_=planes_in)
+
+        quantise_chunk(0)
+
+        w_codes = weights.tile([P, PASSES * D], U32, align_bytes=64)
+        w_scales = weights.tile([P, PASSES * D], U8, align_bytes=64)
+        nc.vector.quantize_mx(out=w_codes[:].bitcast(FP8X4), scales=w_scales[:], in_=w_grouped[:])
+
+        for c in range(1, LOOKAHEAD):
+            transpose_chunk(c)
+        for c in range(1, LOOKAHEAD - 1):
+            quantise_chunk(c)
+
+        for c in range(N_CHUNKS):
+            ahead = c + LOOKAHEAD
+            if ahead < N_CHUNKS:
+                transpose_chunk(ahead)
+            if 0 < ahead - 1 < N_CHUNKS:
+                quantise_chunk(ahead - 1)
+            multiply_chunk(c)

@@ -43,6 +43,7 @@ def tile_hybridsuperlayer_pb_t_kernel(
         const = ctx.enter_context(tc.tile_pool(name="const", bufs=1))
         weights = ctx.enter_context(tc.tile_pool(name="weights", bufs=1))
         h_pool = ctx.enter_context(tc.tile_pool(name="h", bufs=H_BUFS))
+        ordered_pool = ctx.enter_context(tc.tile_pool(name="ordered", bufs=3))
         grouped_pool = ctx.enter_context(tc.tile_pool(name="grouped", bufs=3))
         codes_pool = ctx.enter_context(tc.tile_pool(name="codes", bufs=LOOKAHEAD + 2))
         out_pool = ctx.enter_context(tc.tile_pool(name="outs", bufs=4))
@@ -137,11 +138,26 @@ def tile_hybridsuperlayer_pb_t_kernel(
                 in_=us_grouped[:, g * PACK * P * PACK : (g + 1) * PACK * P * PACK],
             )
 
+        ordered_tiles = {}
         grouped_tiles = {}
         code_tiles = {}
 
+        def order_chunk(c):
+            ordered = ordered_pool.tile([P, TILES * DFF], BF16)
+            words_in = h_tiles[c][:].bitcast(F32).rearrange("p (x q u) -> p x u q", q=P, u=2)
+            words_out = ordered[:].bitcast(F32).rearrange("p (x u q) -> p x u q", q=P, u=2)
+            nc.scalar.copy(out=words_out[:, 0:6], in_=words_in[:, 0:6])
+            nc.vector.tensor_copy(out=words_out[:, 6:8], in_=words_in[:, 6:8])
+            ordered_tiles[c] = ordered
+            load_next(c)
+
+        def load_next(c):
+            if c + H_BUFS < N_CHUNKS:
+                load_chunk(c + H_BUFS)
+
         def transpose_chunk(c):
-            h_words = h_tiles[c][:].bitcast(F32)
+            ordered = c in ordered_tiles
+            h_words = (ordered_tiles[c] if ordered else h_tiles[c])[:].bitcast(F32)
             grouped = grouped_pool.tile([P, CHUNK * PASSES * PACK], BF16, align_bytes=64)
             grouped_words = grouped[:].bitcast(F32).rearrange(
                 "q (i g m u) -> q i g m u", i=TILES, g=PASSES, u=2
@@ -150,18 +166,18 @@ def tile_hybridsuperlayer_pb_t_kernel(
                 xt = xt_pool.tile([P, BANK], F32, tag="xt")
                 for w in range(BANK // P):
                     first = 512 * i + 256 * (w // 2)
-                    nc.tensor.transpose(
-                        xt[:, w * P : (w + 1) * P],
-                        h_words[:, first + w % 2 : first + 256 : 2],
-                        ident[:],
-                    )
+                    if ordered:
+                        words = slice(512 * i + P * w, 512 * i + P * (w + 1))
+                    else:
+                        words = slice(first + w % 2, first + 256, 2)
+                    nc.tensor.transpose(xt[:, w * P : (w + 1) * P], h_words[:, words], ident[:])
                 nc.scalar.copy(
                     out=grouped_words[:, i],
                     in_=xt[:].rearrange("q (g u m) -> q g m u", g=PASSES, u=2),
                 )
             grouped_tiles[c] = grouped
-            if c + H_BUFS < N_CHUNKS:
-                load_chunk(c + H_BUFS)
+            if not ordered:
+                load_next(c)
 
         def quantise_chunk(c):
             h_codes = codes_pool.tile([P, CHUNK * PASSES], U32, align_bytes=64)
@@ -233,11 +249,14 @@ def tile_hybridsuperlayer_pb_t_kernel(
             transpose_chunk(c)
         for c in range(1, LOOKAHEAD - 1):
             quantise_chunk(c)
+        order_chunk(LOOKAHEAD)
 
         for c in range(N_CHUNKS):
             ahead = c + LOOKAHEAD
             if ahead < N_CHUNKS:
                 transpose_chunk(ahead)
+            if ahead + 1 < N_CHUNKS:
+                order_chunk(ahead + 1)
             if 0 < ahead - 1 < N_CHUNKS:
                 quantise_chunk(ahead - 1)
             multiply_chunk(c)

@@ -24,8 +24,11 @@ PASSES = DFF // (P * PACK)
 TILES = 4
 CHUNK = TILES * P
 N_CHUNKS = TOKENS // CHUNK
+UNITS = TILES * PASSES
 
-LOOKAHEAD = 2
+FIRST_ORDERED = 3
+SCALAR_UNITS, VECTOR_UNITS, GPSIMD_UNITS = 5, 3, 0
+FINE_FROM = 14
 H_BUFS = 8
 
 FLOPS = 2 * DFF * R * D + 2 * TOKENS * DFF * D
@@ -43,9 +46,9 @@ def tile_hybridsuperlayer_pb_t_kernel(
         const = ctx.enter_context(tc.tile_pool(name="const", bufs=1))
         weights = ctx.enter_context(tc.tile_pool(name="weights", bufs=1))
         h_pool = ctx.enter_context(tc.tile_pool(name="h", bufs=H_BUFS))
-        ordered_pool = ctx.enter_context(tc.tile_pool(name="ordered", bufs=3))
+        ordered_pool = ctx.enter_context(tc.tile_pool(name="ordered", bufs=4))
         grouped_pool = ctx.enter_context(tc.tile_pool(name="grouped", bufs=3))
-        codes_pool = ctx.enter_context(tc.tile_pool(name="codes", bufs=LOOKAHEAD + 2))
+        codes_pool = ctx.enter_context(tc.tile_pool(name="codes", bufs=5))
         out_pool = ctx.enter_context(tc.tile_pool(name="outs", bufs=4))
         xt_pool = ctx.enter_context(tc.psum_pool(name="xt", bufs=4))
         acc_pool = ctx.enter_context(tc.psum_pool(name="acc", bufs=4))
@@ -57,19 +60,19 @@ def tile_hybridsuperlayer_pb_t_kernel(
         bias_rows = const.tile([P, D], BF16)
         nc.vector.memset(bias_rows[:], 0.0)
 
+        v_sb = weights.tile([P, (D // P) * R], BF16)
+        v_view = v_sb[:].rearrange("p (t r) -> p t r", r=R)
+        v_dram = c_proj_V.rearrange("(t p) r -> p t r", p=P)
+        for half in range(2):
+            rows = slice(2 * half, 2 * half + 2)
+            nc.sync.dma_start(out=v_view[:, rows, :], in_=v_dram[:, rows, :])
         s_quad = const.tile([P, PACK], BF16)
         nc.sync.dma_start(out=s_quad[:], in_=c_proj_S.rearrange("(q t) -> q t", t=PACK))
-
         u_sb = weights.tile([P, PLANES * R], BF16)
         u_view = u_sb[:].rearrange("p (c x) -> p c x", c=4)
         u_dram = c_proj_U.rearrange("(g p h e) r -> g h p (e r)", g=PASSES, h=2, e=2)
         for c in range(4):
             nc.sync.dma_start(out=u_view[:, c, :], in_=u_dram[c // 2, c % 2])
-        v_sb = weights.tile([P, (D // P) * R], BF16)
-        nc.sync.dma_start(
-            out=v_sb[:].rearrange("p (t r) -> p t r", r=R),
-            in_=c_proj_V.rearrange("(t p) r -> p t r", p=P),
-        )
         nc.sync.dma_start(out=bias_rows[0:1, :], in_=c_proj_bias.rearrange("(o d) -> o d", o=1))
 
         h_tiles = {}
@@ -82,8 +85,30 @@ def tile_hybridsuperlayer_pb_t_kernel(
         for c in range(H_BUFS):
             load_chunk(c)
 
+        v_words = v_sb[:].bitcast(F32)
+        v_grouped = weights.tile([P, D * PACK], BF16, align_bytes=64)
+        v_grouped_words = v_grouped[:].bitcast(F32).rearrange("q (d a) -> q d a", a=2)
+        for half in range(2):
+            vt = xt_pool.tile([P, BANK], F32, tag="xt")
+            for s in range(2):
+                for a in range(2):
+                    t = 2 * half + s
+                    nc.tensor.transpose(
+                        vt[:, (2 * a + s) * P : (2 * a + s + 1) * P],
+                        v_words[:, 256 * t + a : 256 * (t + 1) : 2],
+                        ident[:],
+                    )
+            nc.scalar.copy(
+                out=v_grouped_words[:, half * 256 : (half + 1) * 256, :],
+                in_=vt[:].rearrange("q (a d) -> q d a", a=2),
+            )
+        v_codes = weights.tile([P, D], U32, align_bytes=64)
+        v_scales = weights.tile([P, D], U8, align_bytes=64)
+
         u_words = u_sb[:].bitcast(F32)
         us_grouped = weights.tile([P, PLANES * P * PACK], BF16, align_bytes=64)
+        us_codes = weights.tile([P, PLANES * P], U32, align_bytes=64)
+        us_scales = weights.tile([P, PLANES * P], U8, align_bytes=64)
         s_repeated = (
             s_quad[:].rearrange("q (a b) -> q a b", b=2).unsqueeze(1).to_broadcast([P, P, 2, 2])
         )
@@ -107,90 +132,87 @@ def tile_hybridsuperlayer_pb_t_kernel(
                     in1=s_repeated,
                     op=MULT,
                 )
-
-        v_words = v_sb[:].bitcast(F32)
-        v_grouped = weights.tile([P, D * PACK], BF16, align_bytes=64)
-        v_grouped_words = v_grouped[:].bitcast(F32).rearrange("q (d a) -> q d a", a=2)
-        for half in range(2):
-            vt = xt_pool.tile([P, BANK], F32, tag="xt")
-            for a in range(2):
-                for s in range(2):
-                    t = 2 * half + s
-                    nc.tensor.transpose(
-                        vt[:, (2 * a + s) * P : (2 * a + s + 1) * P],
-                        v_words[:, 256 * t + a : 256 * (t + 1) : 2],
-                        ident[:],
-                    )
-            nc.scalar.copy(
-                out=v_grouped_words[:, half * 256 : (half + 1) * 256, :],
-                in_=vt[:].rearrange("q (a d) -> q d a", a=2),
-            )
-
-        v_codes = weights.tile([P, D], U32, align_bytes=64)
-        v_scales = weights.tile([P, D], U8, align_bytes=64)
-        nc.vector.quantize_mx(out=v_codes[:].bitcast(FP8X4), scales=v_scales[:], in_=v_grouped[:])
-        us_codes = weights.tile([P, PLANES * P], U32, align_bytes=64)
-        us_scales = weights.tile([P, PLANES * P], U8, align_bytes=64)
-        for g in range(PASSES):
-            nc.vector.quantize_mx(
-                out=us_codes[:, g * PACK * P : (g + 1) * PACK * P].bitcast(FP8X4),
-                scales=us_scales[:, g * PACK * P : (g + 1) * PACK * P],
-                in_=us_grouped[:, g * PACK * P * PACK : (g + 1) * PACK * P * PACK],
-            )
+            if c == 0:
+                nc.vector.quantize_mx(
+                    out=v_codes[:].bitcast(FP8X4), scales=v_scales[:], in_=v_grouped[:]
+                )
+            if c % 2 == 1:
+                g = c // 2
+                nc.vector.quantize_mx(
+                    out=us_codes[:, g * PACK * P : (g + 1) * PACK * P].bitcast(FP8X4),
+                    scales=us_scales[:, g * PACK * P : (g + 1) * PACK * P],
+                    in_=us_grouped[:, g * PACK * P * PACK : (g + 1) * PACK * P * PACK],
+                )
 
         ordered_tiles = {}
         grouped_tiles = {}
         code_tiles = {}
+        out_tiles = {}
 
-        def order_chunk(c):
-            ordered = ordered_pool.tile([P, TILES * DFF], BF16)
+        def order(c):
+            if not FIRST_ORDERED <= c < N_CHUNKS:
+                return
+            moved = SCALAR_UNITS + VECTOR_UNITS + GPSIMD_UNITS
+            ordered = ordered_pool.tile([P, moved * 512], BF16)
             words_in = h_tiles[c][:].bitcast(F32).rearrange("p (x q u) -> p x u q", q=P, u=2)
             words_out = ordered[:].bitcast(F32).rearrange("p (x u q) -> p x u q", q=P, u=2)
-            nc.scalar.copy(out=words_out[:, 0:6], in_=words_in[:, 0:6])
-            nc.vector.tensor_copy(out=words_out[:, 6:8], in_=words_in[:, 6:8])
-            ordered_tiles[c] = ordered
-            load_next(c)
+            a, b = SCALAR_UNITS, SCALAR_UNITS + VECTOR_UNITS
+            if GPSIMD_UNITS:
+                pairs_in = h_tiles[c][:].rearrange("p (x q u e) -> p x u q e", q=P, u=2, e=2)
+                pairs_out = ordered[:].rearrange("p (x u q e) -> p x u q e", q=P, u=2, e=2)
+                for x in range(b, moved):
+                    nc.gpsimd.tensor_scalar(out=pairs_out[:, x], in0=pairs_in[:, x], scalar1=1.0, scalar2=0.0, op0=MULT, op1=ADD)
+            nc.scalar.copy(out=words_out[:, 0:a], in_=words_in[:, 0:a])
+            if VECTOR_UNITS:
+                nc.vector.tensor_copy(out=words_out[:, a:b], in_=words_in[:, a:b])
+            ordered_tiles[c] = (moved, ordered)
 
-        def load_next(c):
-            if c + H_BUFS < N_CHUNKS:
-                load_chunk(c + H_BUFS)
-
-        def transpose_chunk(c):
-            ordered = c in ordered_tiles
-            h_words = (ordered_tiles[c] if ordered else h_tiles[c])[:].bitcast(F32)
-            grouped = grouped_pool.tile([P, CHUNK * PASSES * PACK], BF16, align_bytes=64)
-            grouped_words = grouped[:].bitcast(F32).rearrange(
+        def transpose(c, first_tile=0, last_tile=TILES):
+            if c >= N_CHUNKS:
+                return
+            moved, ordered = ordered_tiles.get(c, (0, None))
+            if first_tile == 0:
+                grouped = grouped_pool.tile([P, TILES * P * PASSES * PACK], BF16, align_bytes=64)
+                grouped_tiles[c] = grouped
+            grouped_words = grouped_tiles[c][:].bitcast(F32).rearrange(
                 "q (i g m u) -> q i g m u", i=TILES, g=PASSES, u=2
             )
-            for i in range(TILES):
+            for i in range(first_tile, last_tile):
                 xt = xt_pool.tile([P, BANK], F32, tag="xt")
                 for w in range(BANK // P):
-                    first = 512 * i + 256 * (w // 2)
-                    if ordered:
-                        words = slice(512 * i + P * w, 512 * i + P * (w + 1))
+                    unit, u = PASSES * i + w // 2, w % 2
+                    if unit < moved:
+                        first = 256 * unit + P * u
+                        words = ordered[:].bitcast(F32)[:, first : first + P]
                     else:
-                        words = slice(first + w % 2, first + 256, 2)
-                    nc.tensor.transpose(xt[:, w * P : (w + 1) * P], h_words[:, words], ident[:])
+                        words = h_tiles[c][:].bitcast(F32)[:, 256 * unit + u : 256 * (unit + 1) : 2]
+                    nc.tensor.transpose(xt[:, w * P : (w + 1) * P], words, ident[:])
                 nc.scalar.copy(
                     out=grouped_words[:, i],
                     in_=xt[:].rearrange("q (g u m) -> q g m u", g=PASSES, u=2),
                 )
-            grouped_tiles[c] = grouped
-            if not ordered:
-                load_next(c)
+            if last_tile == TILES and c + H_BUFS < N_CHUNKS:
+                load_chunk(c + H_BUFS)
 
-        def quantise_chunk(c):
-            h_codes = codes_pool.tile([P, CHUNK * PASSES], U32, align_bytes=64)
-            h_scales = codes_pool.tile([P, CHUNK * PASSES], U8, align_bytes=64)
+        def quantise(c, first_tile=0, last_tile=TILES):
+            if c >= N_CHUNKS:
+                return
+            if first_tile == 0:
+                h_codes = codes_pool.tile([P, TILES * P * PASSES], U32, align_bytes=64)
+                h_scales = codes_pool.tile([P, TILES * P * PASSES], U8, align_bytes=64)
+                code_tiles[c] = (h_codes, h_scales)
+            codes, scales = code_tiles[c]
+            a, b = first_tile * P * PASSES, last_tile * P * PASSES
             nc.vector.quantize_mx(
-                out=h_codes[:].bitcast(FP8X4), scales=h_scales[:], in_=grouped_tiles[c][:]
+                out=codes[:, a:b].bitcast(FP8X4), scales=scales[:, a:b], in_=grouped_tiles[c][:, a * PACK : b * PACK]
             )
-            code_tiles[c] = (h_codes, h_scales)
 
-        def multiply_chunk(c):
+        def multiply(c, first_tile=0, last_tile=TILES):
             h_codes, h_scales = code_tiles[c]
-            out_sb = out_pool.tile([P, TILES * D], F32)
-            for i in range(TILES):
+            if first_tile == 0:
+                out_sb = out_pool.tile([P, TILES * D], F32)
+                out_tiles[c] = out_sb
+            for i in range(first_tile, last_tile):
                 acc = acc_pool.tile([P, D], F32, tag="acc")
                 for g in range(PASSES):
                     tokens = slice((PASSES * i + g) * P, (PASSES * i + g + 1) * P)
@@ -204,12 +226,12 @@ def tile_hybridsuperlayer_pb_t_kernel(
                         start=(g == 0),
                         stop=(g == PASSES - 1),
                     )
-                nc.vector.tensor_tensor(
-                    out=out_sb[:, i * D : (i + 1) * D], in0=acc[:], in1=bias_bc[:], op=ADD
-                )
-            nc.sync.dma_start(out=out_chunks[c], in_=out_sb[:])
-
-        transpose_chunk(0)
+                cols = slice(i * D, (i + 1) * D)
+                nc.vector.tensor_tensor(out=out_tiles[c][:, cols], in0=acc[:], in1=bias_bc[:], op=ADD)
+                if c >= FINE_FROM:
+                    nc.sync.dma_start(out=out_chunks[c][:, cols], in_=out_tiles[c][:, cols])
+            if c < FINE_FROM and last_tile == TILES:
+                nc.sync.dma_start(out=out_chunks[c], in_=out_tiles[c][:])
 
         bias_ps = acc_pool.tile([P, D], F32, tag="acc")
         nc.tensor.matmul(out=bias_ps[:], lhsT=ones[:], rhs=bias_rows[:], start=True, stop=True)
@@ -217,6 +239,8 @@ def tile_hybridsuperlayer_pb_t_kernel(
         nc.scalar.copy(out=bias_bc[:], in_=bias_ps[:])
 
         w_grouped = weights.tile([P, PASSES * D * PACK], BF16, align_bytes=64)
+        w_codes = weights.tile([P, PASSES * D], U32, align_bytes=64)
+        w_scales = weights.tile([P, PASSES * D], U8, align_bytes=64)
         for g in range(PASSES):
             for block in range(D // P):
                 w_ps = acc_pool.tile([P, BANK], F32, tag="acc")
@@ -238,25 +262,23 @@ def tile_hybridsuperlayer_pb_t_kernel(
                     nc.scalar.copy(out=words_out, in_=planes_in)
                 else:
                     nc.vector.tensor_copy(out=words_out, in_=planes_in)
+            nc.vector.quantize_mx(
+                out=w_codes[:, g * D : (g + 1) * D].bitcast(FP8X4),
+                scales=w_scales[:, g * D : (g + 1) * D],
+                in_=w_grouped[:, g * D * PACK : (g + 1) * D * PACK],
+            )
 
-        quantise_chunk(0)
+        transpose(0)
+        transpose(1)
+        quantise(0)
+        order(3)
+        transpose(2)
+        order(4)
+        quantise(1)
+        multiply(0)
 
-        w_codes = weights.tile([P, PASSES * D], U32, align_bytes=64)
-        w_scales = weights.tile([P, PASSES * D], U8, align_bytes=64)
-        nc.vector.quantize_mx(out=w_codes[:].bitcast(FP8X4), scales=w_scales[:], in_=w_grouped[:])
-
-        for c in range(1, LOOKAHEAD):
-            transpose_chunk(c)
-        for c in range(1, LOOKAHEAD - 1):
-            quantise_chunk(c)
-        order_chunk(LOOKAHEAD)
-
-        for c in range(N_CHUNKS):
-            ahead = c + LOOKAHEAD
-            if ahead < N_CHUNKS:
-                transpose_chunk(ahead)
-            if ahead + 1 < N_CHUNKS:
-                order_chunk(ahead + 1)
-            if 0 < ahead - 1 < N_CHUNKS:
-                quantise_chunk(ahead - 1)
-            multiply_chunk(c)
+        for c in range(1, N_CHUNKS):
+            transpose(c + 2)
+            order(c + 4)
+            quantise(c + 1)
+            multiply(c)

@@ -27,7 +27,7 @@ N_CHUNKS = TOKENS // CHUNK
 UNITS = TILES * PASSES
 
 FIRST_ORDERED = 3
-SCALAR_UNITS, VECTOR_UNITS, GPSIMD_UNITS = 5, 3, 0
+SCALAR_UNITS, VECTOR_UNITS, GPSIMD_UNITS = 5, 2, 0
 FINE_FROM = 14
 H_BUFS = 8
 

@@ -27,7 +27,7 @@ N_CHUNKS = TOKENS // CHUNK
 UNITS = TILES * PASSES
 
 FIRST_ORDERED = 3
-SCALAR_UNITS, VECTOR_UNITS, GPSIMD_UNITS = 5, 2, 0
+SCALAR_UNITS, VECTOR_UNITS, GPSIMD_UNITS = 5, 3, 0
 FINE_FROM = 14
 H_BUFS = 8
 
@@ -163,8 +163,9 @@ def tile_hybridsuperlayer_pb_t_kernel(
                 for x in range(b, moved):
                     nc.gpsimd.tensor_scalar(out=pairs_out[:, x], in0=pairs_in[:, x], scalar1=1.0, scalar2=0.0, op0=MULT, op1=ADD)
             nc.scalar.copy(out=words_out[:, 0:a], in_=words_in[:, 0:a])
-            if VECTOR_UNITS:
-                nc.vector.tensor_copy(out=words_out[:, a:b], in_=words_in[:, a:b])
+            for x in range(a, b, 2):
+                units = slice(x, min(x + 2, b))
+                nc.vector.tensor_copy(out=words_out[:, units], in_=words_in[:, units])
             ordered_tiles[c] = (moved, ordered)
 
         def transpose(c, first_tile=0, last_tile=TILES):

@@ -102,13 +102,13 @@ def tile_hybridsuperlayer_pb_t_kernel(
                 out=v_grouped_words[:, half * 256 : (half + 1) * 256, :],
                 in_=vt[:].rearrange("q (a d) -> q d a", a=2),
             )
-        v_codes = weights.tile([P, D], U32, align_bytes=64)
-        v_scales = weights.tile([P, D], U8, align_bytes=64)
+        v_codes = weights.tile([P, D], U32, align_bytes=256)
+        v_scales = weights.tile([P, D], U8, align_bytes=256)
 
         u_words = u_sb[:].bitcast(F32)
         us_grouped = weights.tile([P, PLANES * P * PACK], BF16, align_bytes=64)
-        us_codes = weights.tile([P, PLANES * P], U32, align_bytes=64)
-        us_scales = weights.tile([P, PLANES * P], U8, align_bytes=64)
+        us_codes = weights.tile([P, PLANES * P], U32, align_bytes=256)
+        us_scales = weights.tile([P, PLANES * P], U8, align_bytes=256)
         s_repeated = (
             s_quad[:].rearrange("q (a b) -> q a b", b=2).unsqueeze(1).to_broadcast([P, P, 2, 2])
         )
@@ -199,8 +199,8 @@ def tile_hybridsuperlayer_pb_t_kernel(
             if c >= N_CHUNKS:
                 return
             if first_tile == 0:
-                h_codes = codes_pool.tile([P, TILES * P * PASSES], U32, align_bytes=64)
-                h_scales = codes_pool.tile([P, TILES * P * PASSES], U8, align_bytes=64)
+                h_codes = codes_pool.tile([P, TILES * P * PASSES], U32, align_bytes=256)
+                h_scales = codes_pool.tile([P, TILES * P * PASSES], U8, align_bytes=256)
                 code_tiles[c] = (h_codes, h_scales)
             codes, scales = code_tiles[c]
             a, b = first_tile * P * PASSES, last_tile * P * PASSES
@@ -240,8 +240,8 @@ def tile_hybridsuperlayer_pb_t_kernel(
         nc.scalar.copy(out=bias_bc[:], in_=bias_ps[:])
 
         w_grouped = weights.tile([P, PASSES * D * PACK], BF16, align_bytes=64)
-        w_codes = weights.tile([P, PASSES * D], U32, align_bytes=64)
-        w_scales = weights.tile([P, PASSES * D], U8, align_bytes=64)
+        w_codes = weights.tile([P, PASSES * D], U32, align_bytes=256)
+        w_scales = weights.tile([P, PASSES * D], U8, align_bytes=256)
         for g in range(PASSES):
             for block in range(D // P):
                 w_ps = acc_pool.tile([P, BANK], F32, tag="acc")

from contextlib import ExitStack

import concourse.mybir as mybir
from concourse.masks import make_identity

F32 = mybir.dt.float32
BF16 = mybir.dt.bfloat16
U32 = mybir.dt.uint32
U8 = mybir.dt.uint8
FP8X4 = mybir.dt.float8_e4m3fn_x4
MULT = mybir.AluOpType.mult
ADD = mybir.AluOpType.add

P = 128
PACK = 4
TOKENS = 4 * 2048
DFF = 1024
R = 512
D = 512

BANK = 512
PLANES = DFF // P
PASSES = DFF // (P * PACK)
TILES = 4
CHUNK = TILES * P
N_CHUNKS = TOKENS // CHUNK
UNITS = TILES * PASSES

FIRST_ORDERED = 3
SCALAR_UNITS, VECTOR_UNITS, GPSIMD_UNITS = 5, 3, 0
FINE_FROM = 14
H_BUFS = 8

FLOPS = 2 * DFF * R * D + 2 * TOKENS * DFF * D


def tile_hybridsuperlayer_pb_t_kernel(
    tc, h_gelu, c_proj_U, c_proj_S, c_proj_V, c_proj_bias, out
):
    nc = tc.nc
    h_chunks = h_gelu.flatten_outer_dims().rearrange("(c p i) k -> c p (i k)", p=P, i=TILES)
    out_chunks = out.flatten_outer_dims().rearrange("(c p i) d -> c p (i d)", p=P, i=TILES)

    with ExitStack() as ctx:
        ctx.enter_context(tc.manual_schedule())
        const = ctx.enter_context(tc.tile_pool(name="const", bufs=1))
        weights = ctx.enter_context(tc.tile_pool(name="weights", bufs=1))
        h_pool = ctx.enter_context(tc.tile_pool(name="h", bufs=H_BUFS))
        ordered_pool = ctx.enter_context(tc.tile_pool(name="ordered", bufs=4))
        grouped_pool = ctx.enter_context(tc.tile_pool(name="grouped", bufs=3))
        codes_pool = ctx.enter_context(tc.tile_pool(name="codes", bufs=5))
        out_pool = ctx.enter_context(tc.tile_pool(name="outs", bufs=4))
        xt_pool = ctx.enter_context(tc.psum_pool(name="xt", bufs=4))
        acc_pool = ctx.enter_context(tc.psum_pool(name="acc", bufs=4))

        ident = const.tile([P, P], F32)
        make_identity(nc, ident[:])
        ones = const.tile([P, P], BF16)
        nc.vector.memset(ones[:], 1.0)
        bias_rows = const.tile([P, D], BF16)
        nc.vector.memset(bias_rows[:], 0.0)

        v_sb = weights.tile([P, (D // P) * R], BF16)
        v_view = v_sb[:].rearrange("p (t r) -> p t r", r=R)
        v_dram = c_proj_V.rearrange("(t p) r -> p t r", p=P)
        for half in range(2):
            rows = slice(2 * half, 2 * half + 2)
            nc.sync.dma_start(out=v_view[:, rows, :], in_=v_dram[:, rows, :])
        s_quad = const.tile([P, PACK], BF16)
        nc.sync.dma_start(out=s_quad[:], in_=c_proj_S.rearrange("(q t) -> q t", t=PACK))
        u_sb = weights.tile([P, PLANES * R], BF16)
        u_view = u_sb[:].rearrange("p (c x) -> p c x", c=4)
        u_dram = c_proj_U.rearrange("(g p h e) r -> g h p (e r)", g=PASSES, h=2, e=2)
        for c in range(4):
            nc.sync.dma_start(out=u_view[:, c, :], in_=u_dram[c // 2, c % 2])
        nc.sync.dma_start(out=bias_rows[0:1, :], in_=c_proj_bias.rearrange("(o d) -> o d", o=1))

        h_tiles = {}

        def load_chunk(c):
            h_sb = h_pool.tile([P, TILES * DFF], BF16)
            nc.sync.dma_start(out=h_sb[:], in_=h_chunks[c])
            h_tiles[c] = h_sb

        for c in range(H_BUFS):
            load_chunk(c)

        v_words = v_sb[:].bitcast(F32)
        v_grouped = weights.tile([P, D * PACK], BF16, align_bytes=64)
        v_grouped_words = v_grouped[:].bitcast(F32).rearrange("q (d a) -> q d a", a=2)
        for half in range(2):
            vt = xt_pool.tile([P, BANK], F32, tag="xt")
            for s in range(2):
                for a in range(2):
                    t = 2 * half + s
                    nc.tensor.transpose(
                        vt[:, (2 * a + s) * P : (2 * a + s + 1) * P],
                        v_words[:, 256 * t + a : 256 * (t + 1) : 2],
                        ident[:],
                    )
            nc.scalar.copy(
                out=v_grouped_words[:, half * 256 : (half + 1) * 256, :],
                in_=vt[:].rearrange("q (a d) -> q d a", a=2),
            )
        v_codes = weights.tile([P, D], U32, align_bytes=256)
        v_scales = weights.tile([P, D], U8, align_bytes=256)

        u_words = u_sb[:].bitcast(F32)
        us_grouped = weights.tile([P, PLANES * P * PACK], BF16, align_bytes=64)
        us_codes = weights.tile([P, PLANES * P], U32, align_bytes=256)
        us_scales = weights.tile([P, PLANES * P], U8, align_bytes=256)
        s_repeated = (
            s_quad[:].rearrange("q (a b) -> q a b", b=2).unsqueeze(1).to_broadcast([P, P, 2, 2])
        )
        for c in range(PLANES // 2):
            ut = xt_pool.tile([P, BANK], F32, tag="xt")
            for e in range(2):
                for a in range(2):
                    nc.tensor.transpose(
                        ut[:, (2 * e + a) * P : (2 * e + a + 1) * P],
                        u_words[:, 256 * (2 * c + e) + a : 256 * (2 * c + e + 1) : 2],
                        ident[:],
                    )
            ut_pairs = ut[:].bitcast(BF16).rearrange("q (e a m b) -> q e m a b", e=2, a=2, b=2)
            for e in range(2):
                j = 2 * c + e
                nc.vector.tensor_tensor(
                    out=us_grouped[:, j * P * PACK : (j + 1) * P * PACK].rearrange(
                        "q (m a b) -> q m a b", a=2, b=2
                    ),
                    in0=ut_pairs[:, e],
                    in1=s_repeated,
                    op=MULT,
                )
            if c == 0:
                nc.vector.quantize_mx(
                    out=v_codes[:].bitcast(FP8X4), scales=v_scales[:], in_=v_grouped[:]
                )
            if c % 2 == 1:
                g = c // 2
                nc.vector.quantize_mx(
                    out=us_codes[:, g * PACK * P : (g + 1) * PACK * P].bitcast(FP8X4),
                    scales=us_scales[:, g * PACK * P : (g + 1) * PACK * P],
                    in_=us_grouped[:, g * PACK * P * PACK : (g + 1) * PACK * P * PACK],
                )

        ordered_tiles = {}
        grouped_tiles = {}
        code_tiles = {}
        out_tiles = {}

        def order(c):
            if not FIRST_ORDERED <= c < N_CHUNKS:
                return
            moved = SCALAR_UNITS + VECTOR_UNITS + GPSIMD_UNITS
            ordered = ordered_pool.tile([P, moved * 512], BF16)
            words_in = h_tiles[c][:].bitcast(F32).rearrange("p (x q u) -> p x u q", q=P, u=2)
            words_out = ordered[:].bitcast(F32).rearrange("p (x u q) -> p x u q", q=P, u=2)
            a, b = SCALAR_UNITS, SCALAR_UNITS + VECTOR_UNITS
            if GPSIMD_UNITS:
                pairs_in = h_tiles[c][:].rearrange("p (x q u e) -> p x u q e", q=P, u=2, e=2)
                pairs_out = ordered[:].rearrange("p (x u q e) -> p x u q e", q=P, u=2, e=2)
                for x in range(b, moved):
                    nc.gpsimd.tensor_scalar(out=pairs_out[:, x], in0=pairs_in[:, x], scalar1=1.0, scalar2=0.0, op0=MULT, op1=ADD)
            nc.scalar.copy(out=words_out[:, 0:a], in_=words_in[:, 0:a])
            for x in range(a, b, 2):
                units = slice(x, min(x + 2, b))
                nc.vector.tensor_copy(out=words_out[:, units], in_=words_in[:, units])
            ordered_tiles[c] = (moved, ordered)

        def transpose(c, first_tile=0, last_tile=TILES):
            if c >= N_CHUNKS:
                return
            moved, ordered = ordered_tiles.get(c, (0, None))
            if first_tile == 0:
                grouped = grouped_pool.tile([P, TILES * P * PASSES * PACK], BF16, align_bytes=64)
                grouped_tiles[c] = grouped
            grouped_words = grouped_tiles[c][:].bitcast(F32).rearrange(
                "q (i g m u) -> q i g m u", i=TILES, g=PASSES, u=2
            )
            for i in range(first_tile, last_tile):
                xt = xt_pool.tile([P, BANK], F32, tag="xt")
                for w in range(BANK // P):
                    unit, u = PASSES * i + w // 2, w % 2
                    if unit < moved:
                        first = 256 * unit + P * u
                        words = ordered[:].bitcast(F32)[:, first : first + P]
                    else:
                        words = h_tiles[c][:].bitcast(F32)[:, 256 * unit + u : 256 * (unit + 1) : 2]
                    nc.tensor.transpose(xt[:, w * P : (w + 1) * P], words, ident[:])
                nc.scalar.copy(
                    out=grouped_words[:, i],
                    in_=xt[:].rearrange("q (g u m) -> q g m u", g=PASSES, u=2),
                )
            if last_tile == TILES and c + H_BUFS < N_CHUNKS:
                load_chunk(c + H_BUFS)

        def quantise(c, first_tile=0, last_tile=TILES):
            if c >= N_CHUNKS:
                return
            if first_tile == 0:
                h_codes = codes_pool.tile([P, TILES * P * PASSES], U32, align_bytes=256)
                h_scales = codes_pool.tile([P, TILES * P * PASSES], U8, align_bytes=256)
                code_tiles[c] = (h_codes, h_scales)
            codes, scales = code_tiles[c]
            a, b = first_tile * P * PASSES, last_tile * P * PASSES
            nc.vector.quantize_mx(
                out=codes[:, a:b].bitcast(FP8X4), scales=scales[:, a:b], in_=grouped_tiles[c][:, a * PACK : b * PACK]
            )

        def multiply(c, first_tile=0, last_tile=TILES):
            h_codes, h_scales = code_tiles[c]
            if first_tile == 0:
                out_sb = out_pool.tile([P, TILES * D], F32)
                out_tiles[c] = out_sb
            for i in range(first_tile, last_tile):
                acc = acc_pool.tile([P, D], F32, tag="acc")
                for g in range(PASSES):
                    tokens = slice((PASSES * i + g) * P, (PASSES * i + g + 1) * P)
                    features = slice(g * D, (g + 1) * D)
                    nc.tensor.matmul_mx(
                        out=acc[:],
                        lhsT=h_codes[:, tokens].bitcast(FP8X4),
                        lhsT_scale=h_scales[:, tokens],
                        rhs=w_codes[:, features].bitcast(FP8X4),
                        rhs_scale=w_scales[:, features],
                        start=(g == 0),
                        stop=(g == PASSES - 1),
                    )
                cols = slice(i * D, (i + 1) * D)
                nc.vector.tensor_tensor(out=out_tiles[c][:, cols], in0=acc[:], in1=bias_bc[:], op=ADD)
                if c >= FINE_FROM:
                    nc.sync.dma_start(out=out_chunks[c][:, cols], in_=out_tiles[c][:, cols])
            if c < FINE_FROM and last_tile == TILES:
                nc.sync.dma_start(out=out_chunks[c], in_=out_tiles[c][:])

        bias_ps = acc_pool.tile([P, D], F32, tag="acc")
        nc.tensor.matmul(out=bias_ps[:], lhsT=ones[:], rhs=bias_rows[:], start=True, stop=True)
        bias_bc = const.tile([P, D], F32)
        nc.scalar.copy(out=bias_bc[:], in_=bias_ps[:])

        w_grouped = weights.tile([P, PASSES * D * PACK], BF16, align_bytes=64)
        w_codes = weights.tile([P, PASSES * D], U32, align_bytes=256)
        w_scales = weights.tile([P, PASSES * D], U8, align_bytes=256)
        for g in range(PASSES):
            for block in range(D // P):
                w_ps = acc_pool.tile([P, BANK], F32, tag="acc")
                for t in range(PACK):
                    j = PACK * g + t
                    nc.tensor.matmul_mx(
                        out=w_ps[:, t * P : (t + 1) * P],
                        lhsT=us_codes[:, j * P : (j + 1) * P].bitcast(FP8X4),
                        lhsT_scale=us_scales[:, j * P : (j + 1) * P],
                        rhs=v_codes[:, block * P : (block + 1) * P].bitcast(FP8X4),
                        rhs_scale=v_scales[:, block * P : (block + 1) * P],
                        start=True,
                        stop=True,
                    )
                first = (g * (D // P) + block) * BANK
                words_out = w_grouped[:, first : first + BANK].rearrange("p (d t) -> p d t", t=PACK)
                planes_in = w_ps[:].rearrange("p (t d) -> p d t", t=PACK)
                if block % 2 == 0:
                    nc.scalar.copy(out=words_out, in_=planes_in)
                else:
                    nc.vector.tensor_copy(out=words_out, in_=planes_in)
            nc.vector.quantize_mx(
                out=w_codes[:, g * D : (g + 1) * D].bitcast(FP8X4),
                scales=w_scales[:, g * D : (g + 1) * D],
                in_=w_grouped[:, g * D * PACK : (g + 1) * D * PACK],
            )

        transpose(0)
        transpose(1)
        quantise(0)
        order(3)
        transpose(2)
        order(4)
        quantise(1)
        multiply(0)

        for c in range(1, N_CHUNKS):
            transpose(c + 2)
            order(c + 4)
            quantise(c + 1)
            multiply(c)
